import numpy as np
import ml_dtypes

BF16 = ml_dtypes.bfloat16


def bf(x):
    return np.asarray(x, np.float32).astype(BF16)


def f32(x):
    return np.asarray(x, np.float32)


def f64(x):
    return np.asarray(x).astype(np.float64)


def striped(idx):
    return np.tile(idx.reshape(-1, 16).T, (8, 1))


V, D, H, N = 256, 128, 256, 128


def sigmoid(v):
    return 1.0 / (1.0 + np.exp(-v))


def setup_inputs():
    return {
        "table": bf(np.random.standard_normal((D, V))),
        "w_i": bf(np.random.standard_normal((D, H)) / np.sqrt(D)),
        "w_o": bf(np.random.standard_normal((D, H)) / np.sqrt(D)),
        "w_u": bf(np.random.standard_normal((D, H)) / np.sqrt(D)),
        "b_i": f32(0.3 * np.random.standard_normal((H, 1))),
        "b_o": f32(0.3 * np.random.standard_normal((H, 1))),
        "b_u": f32(0.3 * np.random.standard_normal((H, 1))),
        "offs": striped(np.random.permutation(np.tile(np.arange(V), 2))[:N]),
    }


def reference(table, w_i, w_o, w_u, b_i, b_o, b_u, offs):
    idx = offs[:16].T.reshape(-1)
    x = f64(table)[:, idx]
    gi = sigmoid(f64(w_i).T @ x + f64(b_i))
    go = sigmoid(f64(w_o).T @ x + f64(b_o))
    gu = np.tanh(f64(w_u).T @ x + f64(b_u))
    return go * np.tanh(gi * gu)

@@ -1,0 +1,65 @@
+import concourse.mybir as mybir
+
+BF16, F32, U16 = mybir.dt.bfloat16, mybir.dt.float32, mybir.dt.uint16
+SIGMOID = mybir.ActivationFunctionType.Sigmoid
+TANH = mybir.ActivationFunctionType.Tanh
+MULT = mybir.AluOpType.mult
+
+P = 128
+V = 256
+H = 256
+N = 128
+BLOCKS = H // P
+
+FLOPS = 2 * P * 3 * H * N
+
+
+def tile_treeencodernet_kernel(tc, table, w_i, w_o, w_u, b_i, b_o, b_u, offs, out):
+    nc = tc.nc
+    with (
+        tc.tile_pool(name="held", bufs=1) as held,
+        tc.tile_pool(name="work", bufs=BLOCKS) as work,
+        tc.psum_pool(name="psum", bufs=BLOCKS) as psum,
+    ):
+        offsets = held.tile([P, N // 16], U16, name="offsets")
+        nc.sync.dma_start(offsets[:], offs)
+        words = held.tile([P, V], BF16, name="words")
+        nc.sync.dma_start(words[:], table)
+        weights_i = held.tile([P, H], BF16, name="weights_i")
+        nc.scalar.dma_start(weights_i[:], w_i)
+        weights_u = held.tile([P, H], BF16, name="weights_u")
+        nc.sync.dma_start(weights_u[:], w_u)
+        weights_o = held.tile([P, H], BF16, name="weights_o")
+        nc.sync.dma_start(weights_o[:], w_o)
+
+        bias_i = held.tile([P, BLOCKS], F32, name="bias_i")
+        bias_u = held.tile([P, BLOCKS], F32, name="bias_u")
+        bias_o = held.tile([P, BLOCKS], F32, name="bias_o")
+        with nc.allow_non_contiguous_dma(reason="a bias of 256 values, one value a partition"):
+            for bias, b_dram in ((bias_i, b_i), (bias_u, b_u), (bias_o, b_o)):
+                nc.scalar.dma_start(bias[:], b_dram.rearrange("(b p) o -> p (b o)", p=P))
+
+        for b in range(BLOCKS):
+            block = slice(b * P, (b + 1) * P)
+
+            proj_i = psum.tile([P, N], F32, name="proj_i")
+            nc.tensor.matmul(proj_i[:], weights_i[:, block], words[:].indirect(offsets[:]), start=True, stop=True)
+            proj_u = psum.tile([P, N], F32, name="proj_u")
+            nc.tensor.matmul(proj_u[:], weights_u[:, block], words[:].indirect(offsets[:]), start=True, stop=True)
+            proj_o = psum.tile([P, N], F32, name="proj_o")
+            nc.tensor.matmul(proj_o[:], weights_o[:, block], words[:].indirect(offsets[:]), start=True, stop=True)
+
+            gate_i = work.tile([P, N], F32, name="gate_i")
+            nc.scalar.activation(gate_i[:], proj_i[:], SIGMOID, bias=bias_i[:, b : b + 1])
+            gate_u = work.tile([P, N], F32, name="gate_u")
+            nc.scalar.activation(gate_u[:], proj_u[:], TANH, bias=bias_u[:, b : b + 1])
+            gate_o = work.tile([P, N], F32, name="gate_o")
+            nc.scalar.activation(gate_o[:], proj_o[:], SIGMOID, bias=bias_o[:, b : b + 1])
+
+            cell = work.tile([P, N], F32, name="cell")
+            nc.vector.tensor_tensor(cell[:], gate_i[:], gate_u[:], MULT)
+            squashed = work.tile([P, N], F32, name="squashed")
+            nc.scalar.activation(squashed[:], cell[:], TANH)
+            hidden = work.tile([P, N], F32, name="hidden")
+            nc.vector.tensor_tensor(hidden[:], gate_o[:], squashed[:], MULT)
+            nc.sync.dma_start(out[block, :], hidden[:])

@@ -39,6 +39,10 @@ def tile_treeencodernet_kernel(tc, table, w_i, w_o, w_u, b_i, b_o, b_u, offs, ou
             for bias, b_dram in ((bias_i, b_i), (bias_u, b_u), (bias_o, b_o)):
                 nc.scalar.dma_start(bias[:], b_dram.rearrange("(b p) o -> p (b o)", p=P))
 
+        scratch = held.tile([P, 1], F32, name="scratch")
+        nc.vector.memset(scratch[:], 0.0)
+        nc.scalar.activation(scratch[:], scratch[:], SIGMOID)
+
         for b in range(BLOCKS):
             block = slice(b * P, (b + 1) * P)
 

@@ -10,6 +10,8 @@ V = 256
 H = 256
 N = 128
 BLOCKS = H // P
+BANK = 512
+WARMING_MATMULS = 4
 
 FLOPS = 2 * P * 3 * H * N
 
@@ -20,6 +22,7 @@ def tile_treeencodernet_kernel(tc, table, w_i, w_o, w_u, b_i, b_o, b_u, offs, ou
         tc.tile_pool(name="held", bufs=1) as held,
         tc.tile_pool(name="work", bufs=BLOCKS) as work,
         tc.psum_pool(name="psum", bufs=BLOCKS) as psum,
+        tc.psum_pool(name="idle", bufs=1) as idle,
     ):
         offsets = held.tile([P, N // 16], U16, name="offsets")
         nc.sync.dma_start(offsets[:], offs)
@@ -39,9 +42,14 @@ def tile_treeencodernet_kernel(tc, table, w_i, w_o, w_u, b_i, b_o, b_u, offs, ou
             for bias, b_dram in ((bias_i, b_i), (bias_u, b_u), (bias_o, b_o)):
                 nc.scalar.dma_start(bias[:], b_dram.rearrange("(b p) o -> p (b o)", p=P))
 
-        scratch = held.tile([P, 1], F32, name="scratch")
-        nc.vector.memset(scratch[:], 0.0)
-        nc.scalar.activation(scratch[:], scratch[:], SIGMOID)
+        zeros = held.tile([P, BANK], BF16, name="zeros")
+        nc.vector.memset(zeros[:], 0.0)
+        table_is_in = held.tile([P, 1], F32, name="table_is_in")
+        nc.scalar.activation(table_is_in[:], zeros[:, 0:1], SIGMOID)
+
+        idle_bank = idle.tile([P, BANK], F32, name="idle_bank")
+        for _ in range(WARMING_MATMULS):
+            nc.tensor.matmul(idle_bank[:], zeros[:, 0:P], zeros[:], start=True, stop=True)
 
         for b in range(BLOCKS):
             block = slice(b * P, (b + 1) * P)

@@ -10,8 +10,7 @@ V = 256
 H = 256
 N = 128
 BLOCKS = H // P
-BANK = 512
-WARMING_MATMULS = 4
+WARMING_MATMULS = 12
 
 FLOPS = 2 * P * 3 * H * N
 
@@ -42,14 +41,14 @@ def tile_treeencodernet_kernel(tc, table, w_i, w_o, w_u, b_i, b_o, b_u, offs, ou
             for bias, b_dram in ((bias_i, b_i), (bias_u, b_u), (bias_o, b_o)):
                 nc.scalar.dma_start(bias[:], b_dram.rearrange("(b p) o -> p (b o)", p=P))
 
-        zeros = held.tile([P, BANK], BF16, name="zeros")
+        zeros = held.tile([P, P], BF16, name="zeros")
         nc.vector.memset(zeros[:], 0.0)
         table_is_in = held.tile([P, 1], F32, name="table_is_in")
         nc.scalar.activation(table_is_in[:], zeros[:, 0:1], SIGMOID)
 
-        idle_bank = idle.tile([P, BANK], F32, name="idle_bank")
-        for _ in range(WARMING_MATMULS):
-            nc.tensor.matmul(idle_bank[:], zeros[:, 0:P], zeros[:], start=True, stop=True)
+        idle_bank = idle.tile([P, P], F32, name="idle_bank")
+        for warming in range(WARMING_MATMULS):
+            nc.tensor.matmul(idle_bank[:], zeros[:], zeros[:], start=True, stop=True)
 
         for b in range(BLOCKS):
             block = slice(b * P, (b + 1) * P)

@@ -1,4 +1,5 @@
 import concourse.mybir as mybir
+from concourse.masks import make_identity
 
 BF16, F32, U16 = mybir.dt.bfloat16, mybir.dt.float32, mybir.dt.uint16
 SIGMOID = mybir.ActivationFunctionType.Sigmoid
@@ -10,7 +11,8 @@ V = 256
 H = 256
 N = 128
 BLOCKS = H // P
-WARMING_MATMULS = 12
+GATES = 3
+GATE_I, GATE_U, GATE_O = 0, 1, 2
 
 FLOPS = 2 * P * 3 * H * N
 
@@ -21,7 +23,7 @@ def tile_treeencodernet_kernel(tc, table, w_i, w_o, w_u, b_i, b_o, b_u, offs, ou
         tc.tile_pool(name="held", bufs=1) as held,
         tc.tile_pool(name="work", bufs=BLOCKS) as work,
         tc.psum_pool(name="psum", bufs=BLOCKS) as psum,
-        tc.psum_pool(name="idle", bufs=1) as idle,
+        tc.psum_pool(name="turned", bufs=1) as turned,
     ):
         offsets = held.tile([P, N // 16], U16, name="offsets")
         nc.sync.dma_start(offsets[:], offs)
@@ -34,21 +36,22 @@ def tile_treeencodernet_kernel(tc, table, w_i, w_o, w_u, b_i, b_o, b_u, offs, ou
         weights_o = held.tile([P, H], BF16, name="weights_o")
         nc.sync.dma_start(weights_o[:], w_o)
 
-        bias_i = held.tile([P, BLOCKS], F32, name="bias_i")
-        bias_u = held.tile([P, BLOCKS], F32, name="bias_u")
-        bias_o = held.tile([P, BLOCKS], F32, name="bias_o")
-        with nc.allow_non_contiguous_dma(reason="a bias of 256 values, one value a partition"):
-            for bias, b_dram in ((bias_i, b_i), (bias_u, b_u), (bias_o, b_o)):
-                nc.scalar.dma_start(bias[:], b_dram.rearrange("(b p) o -> p (b o)", p=P))
+        bias_rows = held.tile([GATES * BLOCKS, P], F32, name="bias_rows")
+        for gate, b_dram in ((GATE_I, b_i), (GATE_U, b_u), (GATE_O, b_o)):
+            nc.scalar.dma_start(
+                bias_rows[gate * BLOCKS : (gate + 1) * BLOCKS, :], b_dram.rearrange("(b p) o -> b (p o)", p=P)
+            )
 
-        zeros = held.tile([P, P], BF16, name="zeros")
-        nc.vector.memset(zeros[:], 0.0)
-        table_is_in = held.tile([P, 1], F32, name="table_is_in")
-        nc.scalar.activation(table_is_in[:], zeros[:, 0:1], SIGMOID)
+        scratch = held.tile([P, 1], F32, name="scratch")
+        nc.vector.memset(scratch[:], 0.0)
+        nc.scalar.activation(scratch[:], scratch[:], SIGMOID)
 
-        idle_bank = idle.tile([P, P], F32, name="idle_bank")
-        for warming in range(WARMING_MATMULS):
-            nc.tensor.matmul(idle_bank[:], zeros[:], zeros[:], start=True, stop=True)
+        identity = held.tile([GATES * BLOCKS, GATES * BLOCKS], F32, name="identity")
+        make_identity(nc, identity[:])
+        bias_bank = turned.tile([P, GATES * BLOCKS], F32, name="bias_bank")
+        nc.tensor.matmul(bias_bank[:], bias_rows[:], identity[:], start=True, stop=True)
+        biases = held.tile([P, GATES * BLOCKS], F32, name="biases")
+        nc.vector.tensor_copy(biases[:], bias_bank[:])
 
         for b in range(BLOCKS):
             block = slice(b * P, (b + 1) * P)
@@ -61,11 +64,11 @@ def tile_treeencodernet_kernel(tc, table, w_i, w_o, w_u, b_i, b_o, b_u, offs, ou
             nc.tensor.matmul(proj_o[:], weights_o[:, block], words[:].indirect(offsets[:]), start=True, stop=True)
 
             gate_i = work.tile([P, N], F32, name="gate_i")
-            nc.scalar.activation(gate_i[:], proj_i[:], SIGMOID, bias=bias_i[:, b : b + 1])
+            nc.scalar.activation(gate_i[:], proj_i[:], SIGMOID, bias=biases[:, GATE_I * BLOCKS + b : GATE_I * BLOCKS + b + 1])
             gate_u = work.tile([P, N], F32, name="gate_u")
-            nc.scalar.activation(gate_u[:], proj_u[:], TANH, bias=bias_u[:, b : b + 1])
+            nc.scalar.activation(gate_u[:], proj_u[:], TANH, bias=biases[:, GATE_U * BLOCKS + b : GATE_U * BLOCKS + b + 1])
             gate_o = work.tile([P, N], F32, name="gate_o")
-            nc.scalar.activation(gate_o[:], proj_o[:], SIGMOID, bias=bias_o[:, b : b + 1])
+            nc.scalar.activation(gate_o[:], proj_o[:], SIGMOID, bias=biases[:, GATE_O * BLOCKS + b : GATE_O * BLOCKS + b + 1])
 
             cell = work.tile([P, N], F32, name="cell")
             nc.vector.tensor_tensor(cell[:], gate_i[:], gate_u[:], MULT)

@@ -1,5 +1,4 @@
 import concourse.mybir as mybir
-from concourse.masks import make_identity
 
 BF16, F32, U16 = mybir.dt.bfloat16, mybir.dt.float32, mybir.dt.uint16
 SIGMOID = mybir.ActivationFunctionType.Sigmoid
@@ -11,8 +10,6 @@ V = 256
 H = 256
 N = 128
 BLOCKS = H // P
-GATES = 3
-GATE_I, GATE_U, GATE_O = 0, 1, 2
 
 FLOPS = 2 * P * 3 * H * N
 
@@ -23,7 +20,6 @@ def tile_treeencodernet_kernel(tc, table, w_i, w_o, w_u, b_i, b_o, b_u, offs, ou
         tc.tile_pool(name="held", bufs=1) as held,
         tc.tile_pool(name="work", bufs=BLOCKS) as work,
         tc.psum_pool(name="psum", bufs=BLOCKS) as psum,
-        tc.psum_pool(name="turned", bufs=1) as turned,
     ):
         offsets = held.tile([P, N // 16], U16, name="offsets")
         nc.sync.dma_start(offsets[:], offs)
@@ -36,44 +32,40 @@ def tile_treeencodernet_kernel(tc, table, w_i, w_o, w_u, b_i, b_o, b_u, offs, ou
         weights_o = held.tile([P, H], BF16, name="weights_o")
         nc.sync.dma_start(weights_o[:], w_o)
 
-        bias_rows = held.tile([GATES * BLOCKS, P], F32, name="bias_rows")
-        for gate, b_dram in ((GATE_I, b_i), (GATE_U, b_u), (GATE_O, b_o)):
-            nc.scalar.dma_start(
-                bias_rows[gate * BLOCKS : (gate + 1) * BLOCKS, :], b_dram.rearrange("(b p) o -> b (p o)", p=P)
-            )
+        bias_i = held.tile([P, BLOCKS], F32, name="bias_i")
+        bias_u = held.tile([P, BLOCKS], F32, name="bias_u")
+        bias_o = held.tile([P, BLOCKS], F32, name="bias_o")
+        with nc.allow_non_contiguous_dma(reason="a bias of 256 values, one value a partition"):
+            for bias, b_dram in ((bias_i, b_i), (bias_u, b_u), (bias_o, b_o)):
+                nc.scalar.dma_start(bias[:], b_dram.rearrange("(b p) o -> p (b o)", p=P))
 
         scratch = held.tile([P, 1], F32, name="scratch")
         nc.vector.memset(scratch[:], 0.0)
         nc.scalar.activation(scratch[:], scratch[:], SIGMOID)
 
-        identity = held.tile([GATES * BLOCKS, GATES * BLOCKS], F32, name="identity")
-        make_identity(nc, identity[:])
-        bias_bank = turned.tile([P, GATES * BLOCKS], F32, name="bias_bank")
-        nc.tensor.matmul(bias_bank[:], bias_rows[:], identity[:], start=True, stop=True)
-        biases = held.tile([P, GATES * BLOCKS], F32, name="biases")
-        nc.vector.tensor_copy(biases[:], bias_bank[:])
-
+        cells = []
         for b in range(BLOCKS):
             block = slice(b * P, (b + 1) * P)
-
             proj_i = psum.tile([P, N], F32, name="proj_i")
             nc.tensor.matmul(proj_i[:], weights_i[:, block], words[:].indirect(offsets[:]), start=True, stop=True)
             proj_u = psum.tile([P, N], F32, name="proj_u")
             nc.tensor.matmul(proj_u[:], weights_u[:, block], words[:].indirect(offsets[:]), start=True, stop=True)
-            proj_o = psum.tile([P, N], F32, name="proj_o")
-            nc.tensor.matmul(proj_o[:], weights_o[:, block], words[:].indirect(offsets[:]), start=True, stop=True)
-
             gate_i = work.tile([P, N], F32, name="gate_i")
-            nc.scalar.activation(gate_i[:], proj_i[:], SIGMOID, bias=biases[:, GATE_I * BLOCKS + b : GATE_I * BLOCKS + b + 1])
+            nc.scalar.activation(gate_i[:], proj_i[:], SIGMOID, bias=bias_i[:, b : b + 1])
             gate_u = work.tile([P, N], F32, name="gate_u")
-            nc.scalar.activation(gate_u[:], proj_u[:], TANH, bias=biases[:, GATE_U * BLOCKS + b : GATE_U * BLOCKS + b + 1])
-            gate_o = work.tile([P, N], F32, name="gate_o")
-            nc.scalar.activation(gate_o[:], proj_o[:], SIGMOID, bias=biases[:, GATE_O * BLOCKS + b : GATE_O * BLOCKS + b + 1])
-
+            nc.scalar.activation(gate_u[:], proj_u[:], TANH, bias=bias_u[:, b : b + 1])
             cell = work.tile([P, N], F32, name="cell")
             nc.vector.tensor_tensor(cell[:], gate_i[:], gate_u[:], MULT)
+            cells.append(cell)
+
+        for b in range(BLOCKS):
+            block = slice(b * P, (b + 1) * P)
+            proj_o = psum.tile([P, N], F32, name="proj_o")
+            nc.tensor.matmul(proj_o[:], weights_o[:, block], words[:].indirect(offsets[:]), start=True, stop=True)
             squashed = work.tile([P, N], F32, name="squashed")
-            nc.scalar.activation(squashed[:], cell[:], TANH)
+            nc.scalar.activation(squashed[:], cells[b][:], TANH)
+            gate_o = work.tile([P, N], F32, name="gate_o")
+            nc.scalar.activation(gate_o[:], proj_o[:], SIGMOID, bias=bias_o[:, b : b + 1])
             hidden = work.tile([P, N], F32, name="hidden")
             nc.vector.tensor_tensor(hidden[:], gate_o[:], squashed[:], MULT)
             nc.sync.dma_start(out[block, :], hidden[:])

@@ -43,6 +43,7 @@ def tile_treeencodernet_kernel(tc, table, w_i, w_o, w_u, b_i, b_o, b_u, offs, ou
         nc.vector.memset(scratch[:], 0.0)
         nc.scalar.activation(scratch[:], scratch[:], SIGMOID)
 
+        halves = (slice(0, N // 2), slice(N // 2, N))
         cells = []
         for b in range(BLOCKS):
             block = slice(b * P, (b + 1) * P)
@@ -53,19 +54,21 @@ def tile_treeencodernet_kernel(tc, table, w_i, w_o, w_u, b_i, b_o, b_u, offs, ou
             gate_i = work.tile([P, N], F32, name="gate_i")
             nc.scalar.activation(gate_i[:], proj_i[:], SIGMOID, bias=bias_i[:, b : b + 1])
             gate_u = work.tile([P, N], F32, name="gate_u")
-            nc.scalar.activation(gate_u[:], proj_u[:], TANH, bias=bias_u[:, b : b + 1])
             cell = work.tile([P, N], F32, name="cell")
-            nc.vector.tensor_tensor(cell[:], gate_i[:], gate_u[:], MULT)
+            for half in halves:
+                nc.scalar.activation(gate_u[:, half], proj_u[:, half], TANH, bias=bias_u[:, b : b + 1])
+                nc.vector.tensor_tensor(cell[:, half], gate_i[:, half], gate_u[:, half], MULT)
             cells.append(cell)
 
         for b in range(BLOCKS):
             block = slice(b * P, (b + 1) * P)
             proj_o = psum.tile([P, N], F32, name="proj_o")
             nc.tensor.matmul(proj_o[:], weights_o[:, block], words[:].indirect(offsets[:]), start=True, stop=True)
-            squashed = work.tile([P, N], F32, name="squashed")
-            nc.scalar.activation(squashed[:], cells[b][:], TANH)
             gate_o = work.tile([P, N], F32, name="gate_o")
             nc.scalar.activation(gate_o[:], proj_o[:], SIGMOID, bias=bias_o[:, b : b + 1])
+            squashed = work.tile([P, N], F32, name="squashed")
             hidden = work.tile([P, N], F32, name="hidden")
-            nc.vector.tensor_tensor(hidden[:], gate_o[:], squashed[:], MULT)
+            for half in halves:
+                nc.scalar.activation(squashed[:, half], cells[b][:, half], TANH)
+                nc.vector.tensor_tensor(hidden[:, half], gate_o[:, half], squashed[:, half], MULT)
             nc.sync.dma_start(out[block, :], hidden[:])

@@ -43,27 +43,30 @@ def tile_treeencodernet_kernel(tc, table, w_i, w_o, w_u, b_i, b_o, b_u, offs, ou
         nc.vector.memset(scratch[:], 0.0)
         nc.scalar.activation(scratch[:], scratch[:], SIGMOID)
 
+        blocks = [slice(b * P, (b + 1) * P) for b in range(BLOCKS)]
+        gates_i = []
+        for b in range(BLOCKS):
+            proj_i = psum.tile([P, N], F32, name="proj_i")
+            nc.tensor.matmul(proj_i[:], weights_i[:, blocks[b]], words[:].indirect(offsets[:]), start=True, stop=True)
+            gate_i = work.tile([P, N], F32, name="gate_i")
+            nc.scalar.activation(gate_i[:], proj_i[:], SIGMOID, bias=bias_i[:, b : b + 1])
+            gates_i.append(gate_i)
+
         halves = (slice(0, N // 2), slice(N // 2, N))
         cells = []
         for b in range(BLOCKS):
-            block = slice(b * P, (b + 1) * P)
-            proj_i = psum.tile([P, N], F32, name="proj_i")
-            nc.tensor.matmul(proj_i[:], weights_i[:, block], words[:].indirect(offsets[:]), start=True, stop=True)
             proj_u = psum.tile([P, N], F32, name="proj_u")
-            nc.tensor.matmul(proj_u[:], weights_u[:, block], words[:].indirect(offsets[:]), start=True, stop=True)
-            gate_i = work.tile([P, N], F32, name="gate_i")
-            nc.scalar.activation(gate_i[:], proj_i[:], SIGMOID, bias=bias_i[:, b : b + 1])
+            nc.tensor.matmul(proj_u[:], weights_u[:, blocks[b]], words[:].indirect(offsets[:]), start=True, stop=True)
             gate_u = work.tile([P, N], F32, name="gate_u")
             cell = work.tile([P, N], F32, name="cell")
             for half in halves:
                 nc.scalar.activation(gate_u[:, half], proj_u[:, half], TANH, bias=bias_u[:, b : b + 1])
-                nc.vector.tensor_tensor(cell[:, half], gate_i[:, half], gate_u[:, half], MULT)
+                nc.vector.tensor_tensor(cell[:, half], gates_i[b][:, half], gate_u[:, half], MULT)
             cells.append(cell)
 
         for b in range(BLOCKS):
-            block = slice(b * P, (b + 1) * P)
             proj_o = psum.tile([P, N], F32, name="proj_o")
-            nc.tensor.matmul(proj_o[:], weights_o[:, block], words[:].indirect(offsets[:]), start=True, stop=True)
+            nc.tensor.matmul(proj_o[:], weights_o[:, blocks[b]], words[:].indirect(offsets[:]), start=True, stop=True)
             gate_o = work.tile([P, N], F32, name="gate_o")
             nc.scalar.activation(gate_o[:], proj_o[:], SIGMOID, bias=bias_o[:, b : b + 1])
             squashed = work.tile([P, N], F32, name="squashed")
@@ -71,4 +74,4 @@ def tile_treeencodernet_kernel(tc, table, w_i, w_o, w_u, b_i, b_o, b_u, offs, ou
             for half in halves:
                 nc.scalar.activation(squashed[:, half], cells[b][:, half], TANH)
                 nc.vector.tensor_tensor(hidden[:, half], gate_o[:, half], squashed[:, half], MULT)
-            nc.sync.dma_start(out[block, :], hidden[:])
+            nc.sync.dma_start(out[blocks[b], :], hidden[:])

@@ -35,15 +35,14 @@ def tile_treeencodernet_kernel(tc, table, w_i, w_o, w_u, b_i, b_o, b_u, offs, ou
         bias_i = held.tile([P, BLOCKS], F32, name="bias_i")
         bias_u = held.tile([P, BLOCKS], F32, name="bias_u")
         bias_o = held.tile([P, BLOCKS], F32, name="bias_o")
-        with nc.allow_non_contiguous_dma(reason="a bias of 256 values, one value a partition"):
-            for bias, b_dram in ((bias_i, b_i), (bias_u, b_u), (bias_o, b_o)):
-                nc.scalar.dma_start(bias[:], b_dram.rearrange("(b p) o -> p (b o)", p=P))
+        for bias, b_dram in ((bias_i, b_i), (bias_u, b_u), (bias_o, b_o)):
+            nc.scalar.dma_start(bias[:], b_dram.rearrange("(p b) o -> p (b o)", b=BLOCKS))
 
         scratch = held.tile([P, 1], F32, name="scratch")
         nc.vector.memset(scratch[:], 0.0)
         nc.scalar.activation(scratch[:], scratch[:], SIGMOID)
 
-        blocks = [slice(b * P, (b + 1) * P) for b in range(BLOCKS)]
+        blocks = [slice(b, H, BLOCKS) for b in range(BLOCKS)]
         gates_i = []
         for b in range(BLOCKS):
             proj_i = psum.tile([P, N], F32, name="proj_i")

@@ -21,10 +21,10 @@ def tile_treeencodernet_kernel(tc, table, w_i, w_o, w_u, b_i, b_o, b_u, offs, ou
         tc.tile_pool(name="work", bufs=BLOCKS) as work,
         tc.psum_pool(name="psum", bufs=BLOCKS) as psum,
     ):
-        offsets = held.tile([P, N // 16], U16, name="offsets")
-        nc.sync.dma_start(offsets[:], offs)
         words = held.tile([P, V], BF16, name="words")
         nc.sync.dma_start(words[:], table)
+        offsets = held.tile([P, N // 16], U16, name="offsets")
+        nc.sync.dma_start(offsets[:], offs)
         weights_i = held.tile([P, H], BF16, name="weights_i")
         nc.scalar.dma_start(weights_i[:], w_i)
         weights_u = held.tile([P, H], BF16, name="weights_u")

@@ -29,14 +29,14 @@ def tile_treeencodernet_kernel(tc, table, w_i, w_o, w_u, b_i, b_o, b_u, offs, ou
         nc.scalar.dma_start(weights_i[:], w_i)
         weights_u = held.tile([P, H], BF16, name="weights_u")
         nc.sync.dma_start(weights_u[:], w_u)
-        weights_o = held.tile([P, H], BF16, name="weights_o")
-        nc.sync.dma_start(weights_o[:], w_o)
 
         bias_i = held.tile([P, BLOCKS], F32, name="bias_i")
         bias_u = held.tile([P, BLOCKS], F32, name="bias_u")
         bias_o = held.tile([P, BLOCKS], F32, name="bias_o")
-        for bias, b_dram in ((bias_i, b_i), (bias_u, b_u), (bias_o, b_o)):
-            nc.scalar.dma_start(bias[:], b_dram.rearrange("(p b) o -> p (b o)", b=BLOCKS))
+        for queue, bias, b_dram in ((nc.scalar, bias_i, b_i), (nc.scalar, bias_u, b_u), (nc.sync, bias_o, b_o)):
+            queue.dma_start(bias[:], b_dram.rearrange("(p b) o -> p (b o)", b=BLOCKS))
+        weights_o = held.tile([P, H], BF16, name="weights_o")
+        nc.scalar.dma_start(weights_o[:], w_o)
 
         scratch = held.tile([P, 1], F32, name="scratch")
         nc.vector.memset(scratch[:], 0.0)

import concourse.mybir as mybir

BF16, F32, U16 = mybir.dt.bfloat16, mybir.dt.float32, mybir.dt.uint16
SIGMOID = mybir.ActivationFunctionType.Sigmoid
TANH = mybir.ActivationFunctionType.Tanh
MULT = mybir.AluOpType.mult

P = 128
V = 256
H = 256
N = 128
BLOCKS = H // P

FLOPS = 2 * P * 3 * H * N


def tile_treeencodernet_kernel(tc, table, w_i, w_o, w_u, b_i, b_o, b_u, offs, out):
    nc = tc.nc
    with (
        tc.tile_pool(name="held", bufs=1) as held,
        tc.tile_pool(name="work", bufs=BLOCKS) as work,
        tc.psum_pool(name="psum", bufs=BLOCKS) as psum,
    ):
        words = held.tile([P, V], BF16, name="words")
        nc.sync.dma_start(words[:], table)
        offsets = held.tile([P, N // 16], U16, name="offsets")
        nc.sync.dma_start(offsets[:], offs)
        weights_i = held.tile([P, H], BF16, name="weights_i")
        nc.scalar.dma_start(weights_i[:], w_i)
        weights_u = held.tile([P, H], BF16, name="weights_u")
        nc.sync.dma_start(weights_u[:], w_u)

        bias_i = held.tile([P, BLOCKS], F32, name="bias_i")
        bias_u = held.tile([P, BLOCKS], F32, name="bias_u")
        bias_o = held.tile([P, BLOCKS], F32, name="bias_o")
        for queue, bias, b_dram in ((nc.scalar, bias_i, b_i), (nc.scalar, bias_u, b_u), (nc.sync, bias_o, b_o)):
            queue.dma_start(bias[:], b_dram.rearrange("(p b) o -> p (b o)", b=BLOCKS))
        weights_o = held.tile([P, H], BF16, name="weights_o")
        nc.scalar.dma_start(weights_o[:], w_o)

        scratch = held.tile([P, 1], F32, name="scratch")
        nc.vector.memset(scratch[:], 0.0)
        nc.scalar.activation(scratch[:], scratch[:], SIGMOID)

        blocks = [slice(b, H, BLOCKS) for b in range(BLOCKS)]
        gates_i = []
        for b in range(BLOCKS):
            proj_i = psum.tile([P, N], F32, name="proj_i")
            nc.tensor.matmul(proj_i[:], weights_i[:, blocks[b]], words[:].indirect(offsets[:]), start=True, stop=True)
            gate_i = work.tile([P, N], F32, name="gate_i")
            nc.scalar.activation(gate_i[:], proj_i[:], SIGMOID, bias=bias_i[:, b : b + 1])
            gates_i.append(gate_i)

        halves = (slice(0, N // 2), slice(N // 2, N))
        cells = []
        for b in range(BLOCKS):
            proj_u = psum.tile([P, N], F32, name="proj_u")
            nc.tensor.matmul(proj_u[:], weights_u[:, blocks[b]], words[:].indirect(offsets[:]), start=True, stop=True)
            gate_u = work.tile([P, N], F32, name="gate_u")
            cell = work.tile([P, N], F32, name="cell")
            for half in halves:
                nc.scalar.activation(gate_u[:, half], proj_u[:, half], TANH, bias=bias_u[:, b : b + 1])
                nc.vector.tensor_tensor(cell[:, half], gates_i[b][:, half], gate_u[:, half], MULT)
            cells.append(cell)

        for b in range(BLOCKS):
            proj_o = psum.tile([P, N], F32, name="proj_o")
            nc.tensor.matmul(proj_o[:], weights_o[:, blocks[b]], words[:].indirect(offsets[:]), start=True, stop=True)
            gate_o = work.tile([P, N], F32, name="gate_o")
            nc.scalar.activation(gate_o[:], proj_o[:], SIGMOID, bias=bias_o[:, b : b + 1])
            squashed = work.tile([P, N], F32, name="squashed")
            hidden = work.tile([P, N], F32, name="hidden")
            for half in halves:
                nc.scalar.activation(squashed[:, half], cells[b][:, half], TANH)
                nc.vector.tensor_tensor(hidden[:, half], gate_o[:, half], squashed[:, half], MULT)
            nc.sync.dma_start(out[blocks[b], :], hidden[:])
